import numpy as np
import ml_dtypes


def mxq(x, axis, fmt="e4m3"):
    dtype, down = {"e4m3": (ml_dtypes.float8_e4m3fn, 7), "e5m2": (ml_dtypes.float8_e5m2, 14)}[fmt]
    v = np.moveaxis(np.asarray(x, np.float32).astype(ml_dtypes.bfloat16).astype(np.float64), axis, -1)
    blocks = v.reshape(v.shape[:-1] + (-1, 32))
    amax = np.abs(blocks).max(-1, keepdims=True)
    byte = np.maximum(np.where(amax > 0, np.frexp(amax)[1] - 1 + 127, 0) - down, 1)
    scale = np.exp2(byte - 127.0)
    codes = (blocks / scale).astype(np.float32).astype(dtype).astype(np.float64)
    return np.moveaxis((codes * scale).reshape(v.shape), -1, axis)


WIDE = False


def mx_kscale(k):
    if not WIDE:
        return np.ones(k)
    levels = np.array([20, -20, 10, -10, 0])
    a = np.random.permutation(np.resize(levels, k // 512 * 4)).reshape(k // 512, 4)
    idx = np.arange(k)
    return np.exp2(a[idx // 512, idx % 128 // 32])


BF16 = ml_dtypes.bfloat16


def bf(x):
    return np.asarray(x, np.float32).astype(BF16)


def f64(x):
    return np.asarray(x).astype(np.float64)


B, S, D, OQ, OKV, R = 2, 256, 1536, 1536, 1536, 128
O = OQ + 2 * OKV

SCALE = 1.0


def setup_inputs():
    u = mx_kscale(O)
    x = np.random.standard_normal((B, S, D))
    W = np.random.standard_normal((O, D)) / np.sqrt(D) / u[:, None]
    b = np.random.standard_normal(O) * 0.5
    A1 = np.random.standard_normal((R, D)) / np.sqrt(D)
    B1 = np.random.standard_normal((OKV, R)) * 0.5 / np.sqrt(R) / u[OQ:OQ + OKV, None]
    A2 = np.random.standard_normal((R, D)) / np.sqrt(D)
    B2 = np.random.standard_normal((OKV, R)) * 0.5 / np.sqrt(R) / u[OQ + OKV:, None]
    g = np.random.standard_normal((B, S, O)) * np.exp2(np.random.randint(-12, 1, (B, S, 1))) * 8.0 * u
    return {"x": bf(x), "W": bf(W), "b": bf(b), "A1": bf(A1), "B1": bf(B1),
            "A2": bf(A2), "B2": bf(B2), "grad_out": bf(g)}


def reference(x, W, b, A1, B1, A2, B2, grad_out):
    gq = mxq(f64(grad_out), 2, "e5m2")
    base = gq @ mxq(f64(W), 0, "e4m3")
    tK = gq[..., OQ:OQ + OKV] @ mxq(f64(B1), 0, "e4m3")
    tV = gq[..., OQ + OKV:] @ mxq(f64(B2), 0, "e4m3")
    return base + SCALE * (tK @ f64(A1) + tV @ f64(A2))

@@ -1,0 +1,274 @@
+from contextlib import ExitStack
+
+import concourse.mybir as mybir
+from concourse.masks import make_identity
+
+F32 = mybir.dt.float32
+BF16 = mybir.dt.bfloat16
+U32 = mybir.dt.uint32
+U8 = mybir.dt.uint8
+E4M3X4 = mybir.dt.float8_e4m3fn_x4
+E5M2X4 = mybir.dt.float8_e5m2_x4
+ADD = mybir.AluOpType.add
+SUB = mybir.AluOpType.subtract
+
+P = 128
+TOK = 512
+O = 4608
+D = 1536
+R = 128
+SEC = 1536
+K_PASS = 512
+N_TILE = 512
+N_BLOCKS = 3
+M_TILES = 4
+PASSES = 9
+CHUNK_ORDER = (3, 4, 5, 6, 7, 8, 0, 1, 2)
+W_BUFS = 6
+HILO = False
+
+FLOPS = 2 * TOK * O * D + 2 * 2 * TOK * SEC * R + 2 * 2 * TOK * R * D
+BYTES = 2 * (O * D + TOK * O + 2 * R * D + 2 * SEC * R) + 4 * TOK * D
+
+
+def tile_kvlora_kernel(tc, x, W, b, A1, B1, A2, B2, grad_out, out):
+    nc = tc.nc
+    g2 = grad_out.flatten_outer_dims()
+    o2 = out.flatten_outer_dims()
+    with ExitStack() as ctx:
+        keep = ctx.enter_context(tc.tile_pool(name="keep", bufs=1))
+        gin = ctx.enter_context(tc.tile_pool(name="gin", bufs=4))
+        ggp = ctx.enter_context(tc.tile_pool(name="ggp", bufs=4))
+        wrawp = ctx.enter_context(tc.tile_pool(name="wrawp", bufs=W_BUFS))
+        wgrpp = ctx.enter_context(tc.tile_pool(name="wgrpp", bufs=4))
+        psa = ctx.enter_context(tc.psum_pool(name="psa", bufs=5))
+        pst = ctx.enter_context(tc.psum_pool(name="pst", bufs=3))
+
+        ident = keep.tile([P, P], F32, name="ident")
+        make_identity(nc, ident[:])
+
+        gq = keep.tile([P, PASSES, TOK], U32, name="gq", align_bytes=64)
+        gs = keep.tile([P, PASSES, TOK], U8, name="gs", align_bytes=64)
+        wq = keep.tile([P, N_BLOCKS * PASSES, N_TILE], U32, name="wq", align_bytes=64)
+        ws = keep.tile([P, N_BLOCKS * PASSES, N_TILE], U8, name="ws", align_bytes=64)
+        braw = keep.tile([P, 6, 4, R], BF16, name="braw")
+        bgrp = keep.tile([P, 6, R, 4], BF16, name="bgrp", align_bytes=64)
+        bq = keep.tile([P, 6, R], U32, name="bq", align_bytes=64)
+        bs = keep.tile([P, 6, R], U8, name="bs", align_bytes=64)
+        ab = keep.tile([P, 2, D], BF16, name="ab")
+        lora = keep.tile([P, M_TILES, D], F32, name="lora")
+
+        def copy_on(on_vector, dst, src):
+            if on_vector:
+                nc.vector.tensor_copy(out=dst, in_=src)
+            else:
+                nc.scalar.copy(out=dst, in_=src)
+
+        def regroup(on_vector, dst, src):
+            copy_on(
+                on_vector,
+                dst.rearrange("p (c i) t -> p c t i", i=4),
+                src.rearrange("p t (c i) -> p c t i", i=4),
+            )
+
+        g_tiles = {}
+
+        def load_g(sec, mp):
+            gt = gin.tile([P, 2, SEC], BF16, name="gt", tag="gt")
+            nc.sync.dma_start(
+                out=gt[:],
+                in_=g2[256 * mp : 256 * mp + 256, SEC * sec : SEC * sec + SEC].rearrange(
+                    "(m p) c -> p m c", p=P
+                ),
+            )
+            g_tiles[(sec, mp)] = gt
+
+        def load_b(which, bmat):
+            nc.sync.dma_start(
+                out=braw[:, 3 * which : 3 * which + 3].rearrange("p c (u e) r -> p (c u) (e r)", e=2),
+                in_=bmat.rearrange("(cu p e) r -> p cu (e r)", p=P, e=2),
+            )
+
+        pieces = [(n, c) for n in range(N_BLOCKS) for c in CHUNK_ORDER]
+        w_tiles = {}
+
+        def load_w(i):
+            n, c = pieces[i]
+            wt = wrawp.tile([P, 4, N_TILE], BF16, name="wt", tag="wt")
+            for e in range(2):
+                nc.sync.dma_start(
+                    out=wt[:, e::2, :],
+                    in_=W[
+                        K_PASS * c + e : K_PASS * (c + 1) : 2, N_TILE * n : N_TILE * (n + 1)
+                    ].rearrange("(u p) w -> p u w", u=2),
+                )
+            w_tiles[i] = wt
+
+        load_g(1, 0)
+        load_g(1, 1)
+        load_b(0, B1)
+        nc.sync.dma_start(out=ab[:, 0, :], in_=A1)
+        load_g(2, 0)
+        load_g(2, 1)
+        load_b(1, B2)
+        nc.sync.dma_start(out=ab[:, 1, :], in_=A2)
+        for i in range(W_BUFS):
+            load_w(i)
+
+        evac_count = [0]
+
+        def g_section(sec):
+            for mp in range(2):
+                gf = g_tiles[(sec, mp)][:].bitcast(F32)
+                for cl in range(3):
+                    c = 3 * sec + cl
+                    xt = pst.tile([P, 2, 2, P], F32, name="xt", tag="tmp")
+                    for mi in range(2):
+                        for u in range(2):
+                            nc.tensor.transpose(
+                                xt[:, mi, u, :],
+                                gf[:, mi, 256 * cl + 128 * u : 256 * cl + 128 * u + 128],
+                                ident[:],
+                            )
+                    gg = ggp.tile([P, 256, 4], BF16, name="gg", tag="gg", align_bytes=64)
+                    copy_on(
+                        evac_count[0] % 3 == 2,
+                        gg[:].bitcast(F32).rearrange("p (m t) u -> p m t u", m=2),
+                        xt[:].rearrange("p m u t -> p m t u"),
+                    )
+                    evac_count[0] += 1
+                    nc.vector.quantize_mx(
+                        out=gq[:, c, 256 * mp : 256 * mp + 256].bitcast(E5M2X4),
+                        scales=gs[:, c, 256 * mp : 256 * mp + 256],
+                        in_=gg[:].rearrange("p t j -> p (t j)"),
+                    )
+
+        def b_section(which):
+            for cl in range(3):
+                j = 3 * which + cl
+                regroup(True, bgrp[:, j], braw[:, j])
+            for cl in range(3):
+                j = 3 * which + cl
+                nc.vector.quantize_mx(
+                    out=bq[:, j, :].bitcast(E4M3X4),
+                    scales=bs[:, j, :],
+                    in_=bgrp[:, j].rearrange("p r t -> p (r t)"),
+                )
+
+        plain_ops = {}
+
+        def lora_mx(which):
+            tt = pst.tile([P, TOK], F32, name="tt", tag="tmp")
+            for cl in range(3):
+                j = 3 * which + cl
+                c = 3 + j
+                nc.tensor.matmul_mx(
+                    out=tt[:],
+                    lhsT=bq[:, j, :].bitcast(E4M3X4),
+                    lhsT_scale=bs[:, j, :],
+                    rhs=gq[:, c, :].bitcast(E5M2X4),
+                    rhs_scale=gs[:, c, :],
+                    start=(cl == 0),
+                    stop=(cl == 2),
+                )
+            if HILO:
+                thi = keep.tile([P, TOK], BF16, name="thi%d" % which)
+                tlo = keep.tile([P, TOK], BF16, name="tlo%d" % which)
+                nc.scalar.copy(out=thi[:], in_=tt[:])
+                nc.vector.tensor_tensor(out=tlo[:], in0=tt[:], in1=thi[:], op=SUB)
+                plain_ops[which] = [(thi, ab[:, which, :]), (tlo, ab[:, which, :])]
+            else:
+                tsb = keep.tile([P, TOK], F32, name="tsb%d" % which)
+                af = keep.tile([P, D], F32, name="af%d" % which)
+                nc.scalar.copy(out=af[:], in_=ab[:, which, :])
+                nc.vector.tensor_copy(out=tsb[:], in_=tt[:])
+                plain_ops[which] = [(tsb, af[:])]
+
+        def plain_part(ps, which, m, n, first, last):
+            ops = plain_ops[which]
+            for idx, (lt, rt) in enumerate(ops):
+                nc.tensor.matmul(
+                    ps[:],
+                    lhsT=lt[:, P * m : P * m + P],
+                    rhs=rt[:, N_TILE * n : N_TILE * n + N_TILE],
+                    start=(first and idx == 0),
+                    stop=(last and idx == len(ops) - 1),
+                )
+
+        def plain_evac(ps, m, n):
+            nc.scalar.copy(out=lora[:, m, N_TILE * n : N_TILE * n + N_TILE], in_=ps[:])
+
+        def plain_tile(m, n):
+            ps = pst.tile([P, N_TILE], F32, name="ps", tag="tmp")
+            plain_part(ps, 0, m, n, True, False)
+            plain_part(ps, 1, m, n, False, True)
+            plain_evac(ps, m, n)
+
+        g_section(1)
+        b_section(0)
+        lora_mx(0)
+        load_g(0, 0)
+        load_g(0, 1)
+        ps0 = []
+        for m in range(M_TILES):
+            ps = psa.tile([P, N_TILE], F32, name="ps0", tag="acc")
+            plain_part(ps, 0, m, 0, True, False)
+            ps0.append(ps)
+        g_section(2)
+        b_section(1)
+        lora_mx(1)
+        for m in range(M_TILES):
+            plain_part(ps0[m], 1, m, 0, False, True)
+            plain_evac(ps0[m], m, 0)
+
+        n_pieces = len(pieces)
+        grp_tiles = {}
+        acc = {}
+
+        def stage_regroup(i):
+            wg = wgrpp.tile([P, N_TILE, 4], BF16, name="wg", tag="wg", align_bytes=64)
+            regroup(i % 2 == 0, wg[:], w_tiles[i][:])
+            grp_tiles[i] = wg
+            if i + W_BUFS < n_pieces:
+                load_w(i + W_BUFS)
+
+        def stage_quant(i):
+            nc.vector.quantize_mx(
+                out=wq[:, i, :].bitcast(E4M3X4),
+                scales=ws[:, i, :],
+                in_=grp_tiles[i][:].rearrange("p w t -> p (w t)"),
+            )
+
+        def stage_mm(i):
+            n, c = pieces[i]
+            k = i % PASSES
+            for m in range(M_TILES):
+                if k == 0:
+                    acc[m] = psa.tile([P, N_TILE], F32, name="acc", tag="acc")
+                nc.tensor.matmul_mx(
+                    out=acc[m][:],
+                    lhsT=gq[:, c, P * m : P * m + P].bitcast(E5M2X4),
+                    lhsT_scale=gs[:, c, P * m : P * m + P],
+                    rhs=wq[:, i, :].bitcast(E4M3X4),
+                    rhs_scale=ws[:, i, :],
+                    start=(k == 0),
+                    stop=(k == PASSES - 1),
+                )
+            if k == PASSES - 1:
+                for m in range(M_TILES):
+                    sl = lora[:, m, N_TILE * n : N_TILE * n + N_TILE]
+                    nc.vector.tensor_tensor(out=sl, in0=acc[m][:], in1=sl, op=ADD)
+                    nc.sync.dma_start(
+                        out=o2[P * m : P * m + P, N_TILE * n : N_TILE * n + N_TILE], in_=sl
+                    )
+            elif n + 1 < N_BLOCKS and k % 2 == 1:
+                plain_tile(k // 2, n + 1)
+
+        for i in range(n_pieces + 1):
+            if i == 5:
+                g_section(0)
+            if i < n_pieces:
+                stage_regroup(i)
+            if i >= 1:
+                stage_quant(i - 1)
+                stage_mm(i - 1)

@@ -57,6 +57,13 @@ def tile_kvlora_kernel(tc, x, W, b, A1, B1, A2, B2, grad_out, out):
         bs = keep.tile([P, 6, R], U8, name="bs", align_bytes=64)
         ab = keep.tile([P, 2, D], BF16, name="ab")
         lora = keep.tile([P, M_TILES, D], F32, name="lora")
+        af = keep.tile([P, 2, D], F32, name="af")
+
+        def cast_a(which, n):
+            nc.scalar.copy(
+                out=af[:, which, N_TILE * n : N_TILE * n + N_TILE],
+                in_=ab[:, which, N_TILE * n : N_TILE * n + N_TILE],
+            )
 
         def copy_on(on_vector, dst, src):
             if on_vector:
@@ -179,10 +186,9 @@ def tile_kvlora_kernel(tc, x, W, b, A1, B1, A2, B2, grad_out, out):
                 plain_ops[which] = [(thi, ab[:, which, :]), (tlo, ab[:, which, :])]
             else:
                 tsb = keep.tile([P, TOK], F32, name="tsb%d" % which)
-                af = keep.tile([P, D], F32, name="af%d" % which)
-                nc.scalar.copy(out=af[:], in_=ab[:, which, :])
-                nc.vector.tensor_copy(out=tsb[:], in_=tt[:])
-                plain_ops[which] = [(tsb, af[:])]
+                nc.vector.tensor_copy(out=tsb[:, 0:P], in_=tt[:, 0:P])
+                nc.vector.tensor_copy(out=tsb[:, P:TOK], in_=tt[:, P:TOK])
+                plain_ops[which] = [(tsb, af[:, which, :])]
 
         def plain_part(ps, which, m, n, first, last):
             ops = plain_ops[which]
@@ -206,24 +212,28 @@ def tile_kvlora_kernel(tc, x, W, b, A1, B1, A2, B2, grad_out, out):
 
         g_section(1)
         b_section(0)
+        cast_a(0, 0)
         lora_mx(0)
         load_g(0, 0)
         load_g(0, 1)
+        g_section(2)
+        b_section(1)
+        cast_a(1, 0)
+        lora_mx(1)
         ps0 = []
         for m in range(M_TILES):
             ps = psa.tile([P, N_TILE], F32, name="ps0", tag="acc")
             plain_part(ps, 0, m, 0, True, False)
             ps0.append(ps)
-        g_section(2)
-        b_section(1)
-        lora_mx(1)
         for m in range(M_TILES):
             plain_part(ps0[m], 1, m, 0, False, True)
             plain_evac(ps0[m], m, 0)
+        for n in range(1, N_BLOCKS):
+            cast_a(0, n)
+            cast_a(1, n)
 
         n_pieces = len(pieces)
         grp_tiles = {}
-        acc = {}
 
         def stage_regroup(i):
             wg = wgrpp.tile([P, N_TILE, 4], BF16, name="wg", tag="wg", align_bytes=64)
@@ -239,36 +249,36 @@ def tile_kvlora_kernel(tc, x, W, b, A1, B1, A2, B2, grad_out, out):
                 in_=grp_tiles[i][:].rearrange("p w t -> p (w t)"),
             )
 
-        def stage_mm(i):
-            n, c = pieces[i]
-            k = i % PASSES
-            for m in range(M_TILES):
-                if k == 0:
-                    acc[m] = psa.tile([P, N_TILE], F32, name="acc", tag="acc")
-                nc.tensor.matmul_mx(
-                    out=acc[m][:],
-                    lhsT=gq[:, c, P * m : P * m + P].bitcast(E5M2X4),
-                    lhsT_scale=gs[:, c, P * m : P * m + P],
-                    rhs=wq[:, i, :].bitcast(E4M3X4),
-                    rhs_scale=ws[:, i, :],
-                    start=(k == 0),
-                    stop=(k == PASSES - 1),
-                )
-            if k == PASSES - 1:
-                for m in range(M_TILES):
-                    sl = lora[:, m, N_TILE * n : N_TILE * n + N_TILE]
-                    nc.vector.tensor_tensor(out=sl, in0=acc[m][:], in1=sl, op=ADD)
-                    nc.sync.dma_start(
-                        out=o2[P * m : P * m + P, N_TILE * n : N_TILE * n + N_TILE], in_=sl
-                    )
-            elif n + 1 < N_BLOCKS and k % 2 == 1:
-                plain_tile(k // 2, n + 1)
-
+        rest = [(m, n) for n in range(1, N_BLOCKS) for m in range(M_TILES)]
         for i in range(n_pieces + 1):
-            if i == 5:
+            if i == 4:
                 g_section(0)
             if i < n_pieces:
                 stage_regroup(i)
             if i >= 1:
                 stage_quant(i - 1)
-                stage_mm(i - 1)
+            if i % 2 == 1 and i // 2 < len(rest):
+                plain_tile(rest[i // 2][0], rest[i // 2][1])
+
+        for n in range(N_BLOCKS):
+            for m in range(M_TILES):
+                acc = psa.tile([P, N_TILE], F32, name="acc", tag="acc")
+                for k in range(PASSES):
+                    i = PASSES * n + k
+                    c = pieces[i][1]
+                    nc.tensor.matmul_mx(
+                        out=acc[:],
+                        lhsT=gq[:, c, P * m : P * m + P].bitcast(E5M2X4),
+                        lhsT_scale=gs[:, c, P * m : P * m + P],
+                        rhs=wq[:, i, :].bitcast(E4M3X4),
+                        rhs_scale=ws[:, i, :],
+                        start=(k == 0),
+                        stop=(k == PASSES - 1),
+                    )
+                halves = 2 if (n == N_BLOCKS - 1 and m == M_TILES - 1) else 1
+                wdt = N_TILE // halves
+                for h in range(halves):
+                    lo = N_TILE * n + wdt * h
+                    sl = lora[:, m, lo : lo + wdt]
+                    nc.vector.tensor_tensor(out=sl, in0=acc[:, wdt * h : wdt * h + wdt], in1=sl, op=ADD)
+                    nc.sync.dma_start(out=o2[P * m : P * m + P, lo : lo + wdt], in_=sl)

@@ -41,8 +41,8 @@ def tile_kvlora_kernel(tc, x, W, b, A1, B1, A2, B2, grad_out, out):
         ggp = ctx.enter_context(tc.tile_pool(name="ggp", bufs=4))
         wrawp = ctx.enter_context(tc.tile_pool(name="wrawp", bufs=W_BUFS))
         wgrpp = ctx.enter_context(tc.tile_pool(name="wgrpp", bufs=4))
-        psa = ctx.enter_context(tc.psum_pool(name="psa", bufs=5))
-        pst = ctx.enter_context(tc.psum_pool(name="pst", bufs=3))
+        psa = ctx.enter_context(tc.psum_pool(name="psa", bufs=8))
+        pst = psa
 
         ident = keep.tile([P, P], F32, name="ident")
         make_identity(nc, ident[:])
@@ -114,11 +114,13 @@ def tile_kvlora_kernel(tc, x, W, b, A1, B1, A2, B2, grad_out, out):
         load_g(1, 0)
         load_g(1, 1)
         load_b(0, B1)
-        nc.sync.dma_start(out=ab[:, 0, :], in_=A1)
+        nc.sync.dma_start(out=ab[:, 0, 0:N_TILE], in_=A1[:, 0:N_TILE])
         load_g(2, 0)
         load_g(2, 1)
         load_b(1, B2)
-        nc.sync.dma_start(out=ab[:, 1, :], in_=A2)
+        nc.sync.dma_start(out=ab[:, 1, 0:N_TILE], in_=A2[:, 0:N_TILE])
+        nc.sync.dma_start(out=ab[:, 0, N_TILE:D], in_=A1[:, N_TILE:D])
+        nc.sync.dma_start(out=ab[:, 1, N_TILE:D], in_=A2[:, N_TILE:D])
         for i in range(W_BUFS):
             load_w(i)
 
@@ -129,7 +131,7 @@ def tile_kvlora_kernel(tc, x, W, b, A1, B1, A2, B2, grad_out, out):
                 gf = g_tiles[(sec, mp)][:].bitcast(F32)
                 for cl in range(3):
                     c = 3 * sec + cl
-                    xt = pst.tile([P, 2, 2, P], F32, name="xt", tag="tmp")
+                    xt = pst.tile([P, 2, 2, P], F32, name="xt", tag="bank")
                     for mi in range(2):
                         for u in range(2):
                             nc.tensor.transpose(
@@ -165,7 +167,7 @@ def tile_kvlora_kernel(tc, x, W, b, A1, B1, A2, B2, grad_out, out):
         plain_ops = {}
 
         def lora_mx(which):
-            tt = pst.tile([P, TOK], F32, name="tt", tag="tmp")
+            tt = pst.tile([P, TOK], F32, name="tt", tag="bank")
             for cl in range(3):
                 j = 3 * which + cl
                 c = 3 + j
@@ -205,7 +207,7 @@ def tile_kvlora_kernel(tc, x, W, b, A1, B1, A2, B2, grad_out, out):
             nc.scalar.copy(out=lora[:, m, N_TILE * n : N_TILE * n + N_TILE], in_=ps[:])
 
         def plain_tile(m, n):
-            ps = pst.tile([P, N_TILE], F32, name="ps", tag="tmp")
+            ps = pst.tile([P, N_TILE], F32, name="ps", tag="bank")
             plain_part(ps, 0, m, n, True, False)
             plain_part(ps, 1, m, n, False, True)
             plain_evac(ps, m, n)
@@ -222,7 +224,7 @@ def tile_kvlora_kernel(tc, x, W, b, A1, B1, A2, B2, grad_out, out):
         lora_mx(1)
         ps0 = []
         for m in range(M_TILES):
-            ps = psa.tile([P, N_TILE], F32, name="ps0", tag="acc")
+            ps = psa.tile([P, N_TILE], F32, name="ps0", tag="bank")
             plain_part(ps, 0, m, 0, True, False)
             ps0.append(ps)
         for m in range(M_TILES):
@@ -262,7 +264,7 @@ def tile_kvlora_kernel(tc, x, W, b, A1, B1, A2, B2, grad_out, out):
 
         for n in range(N_BLOCKS):
             for m in range(M_TILES):
-                acc = psa.tile([P, N_TILE], F32, name="acc", tag="acc")
+                acc = psa.tile([P, N_TILE], F32, name="acc", tag="bank")
                 for k in range(PASSES):
                     i = PASSES * n + k
                     c = pieces[i][1]

@@ -10,7 +10,6 @@ U8 = mybir.dt.uint8
 E4M3X4 = mybir.dt.float8_e4m3fn_x4
 E5M2X4 = mybir.dt.float8_e5m2_x4
 ADD = mybir.AluOpType.add
-SUB = mybir.AluOpType.subtract
 
 P = 128
 TOK = 512
@@ -25,10 +24,15 @@ M_TILES = 4
 PASSES = 9
 CHUNK_ORDER = (3, 4, 5, 6, 7, 8, 0, 1, 2)
 W_BUFS = 6
-HILO = False
+Q_LAG = 3
+PINNED = True
 
 FLOPS = 2 * TOK * O * D + 2 * 2 * TOK * SEC * R + 2 * 2 * TOK * R * D
 BYTES = 2 * (O * D + TOK * O + 2 * R * D + 2 * SEC * R) + 4 * TOK * D
+
+
+def on_scalar(i):
+    return i % 5 in (1, 3)
 
 
 def tile_kvlora_kernel(tc, x, W, b, A1, B1, A2, B2, grad_out, out):
@@ -36,13 +40,14 @@ def tile_kvlora_kernel(tc, x, W, b, A1, B1, A2, B2, grad_out, out):
     g2 = grad_out.flatten_outer_dims()
     o2 = out.flatten_outer_dims()
     with ExitStack() as ctx:
+        if PINNED:
+            ctx.enter_context(tc.manual_schedule())
         keep = ctx.enter_context(tc.tile_pool(name="keep", bufs=1))
-        gin = ctx.enter_context(tc.tile_pool(name="gin", bufs=4))
-        ggp = ctx.enter_context(tc.tile_pool(name="ggp", bufs=4))
+        gin = ctx.enter_context(tc.tile_pool(name="gin", bufs=3))
+        ggp = ctx.enter_context(tc.tile_pool(name="ggp", bufs=6))
         wrawp = ctx.enter_context(tc.tile_pool(name="wrawp", bufs=W_BUFS))
-        wgrpp = ctx.enter_context(tc.tile_pool(name="wgrpp", bufs=4))
-        psa = ctx.enter_context(tc.psum_pool(name="psa", bufs=8))
-        pst = psa
+        wgrpp = ctx.enter_context(tc.tile_pool(name="wgrpp", bufs=Q_LAG + 2))
+        psum = ctx.enter_context(tc.psum_pool(name="psum", bufs=8))
 
         ident = keep.tile([P, P], F32, name="ident")
         make_identity(nc, ident[:])
@@ -56,27 +61,17 @@ def tile_kvlora_kernel(tc, x, W, b, A1, B1, A2, B2, grad_out, out):
         bq = keep.tile([P, 6, R], U32, name="bq", align_bytes=64)
         bs = keep.tile([P, 6, R], U8, name="bs", align_bytes=64)
         ab = keep.tile([P, 2, D], BF16, name="ab")
-        lora = keep.tile([P, M_TILES, D], F32, name="lora")
         af = keep.tile([P, 2, D], F32, name="af")
-
-        def cast_a(which, n):
-            nc.scalar.copy(
-                out=af[:, which, N_TILE * n : N_TILE * n + N_TILE],
-                in_=ab[:, which, N_TILE * n : N_TILE * n + N_TILE],
-            )
-
-        def copy_on(on_vector, dst, src):
-            if on_vector:
-                nc.vector.tensor_copy(out=dst, in_=src)
-            else:
-                nc.scalar.copy(out=dst, in_=src)
+        tsb = keep.tile([P, 2, TOK], F32, name="tsb")
+        lora = keep.tile([P, M_TILES, D], F32, name="lora")
 
         def regroup(on_vector, dst, src):
-            copy_on(
-                on_vector,
-                dst.rearrange("p (c i) t -> p c t i", i=4),
-                src.rearrange("p t (c i) -> p c t i", i=4),
-            )
+            dv = dst.rearrange("p (c i) t -> p c t i", i=4)
+            sv = src.rearrange("p t (c i) -> p c t i", i=4)
+            if on_vector:
+                nc.vector.tensor_copy(out=dv, in_=sv)
+            else:
+                nc.scalar.copy(out=dv, in_=sv)
 
         g_tiles = {}
 
@@ -96,7 +91,11 @@ def tile_kvlora_kernel(tc, x, W, b, A1, B1, A2, B2, grad_out, out):
                 in_=bmat.rearrange("(cu p e) r -> p cu (e r)", p=P, e=2),
             )
 
+        def load_a(which, amat, lo, hi):
+            nc.sync.dma_start(out=ab[:, which, lo:hi], in_=amat[:, lo:hi])
+
         pieces = [(n, c) for n in range(N_BLOCKS) for c in CHUNK_ORDER]
+        n_pieces = len(pieces)
         w_tiles = {}
 
         def load_w(i):
@@ -111,51 +110,44 @@ def tile_kvlora_kernel(tc, x, W, b, A1, B1, A2, B2, grad_out, out):
                 )
             w_tiles[i] = wt
 
-        load_g(1, 0)
-        load_g(1, 1)
-        load_b(0, B1)
-        nc.sync.dma_start(out=ab[:, 0, 0:N_TILE], in_=A1[:, 0:N_TILE])
-        load_g(2, 0)
-        load_g(2, 1)
-        load_b(1, B2)
-        nc.sync.dma_start(out=ab[:, 1, 0:N_TILE], in_=A2[:, 0:N_TILE])
-        nc.sync.dma_start(out=ab[:, 0, N_TILE:D], in_=A1[:, N_TILE:D])
-        nc.sync.dma_start(out=ab[:, 1, N_TILE:D], in_=A2[:, N_TILE:D])
-        for i in range(W_BUFS):
-            load_w(i)
+        def cast_a(which, n):
+            nc.scalar.copy(
+                out=af[:, which, N_TILE * n : N_TILE * n + N_TILE],
+                in_=ab[:, which, N_TILE * n : N_TILE * n + N_TILE],
+            )
 
-        evac_count = [0]
+        gg_tiles = {}
 
-        def g_section(sec):
-            for mp in range(2):
-                gf = g_tiles[(sec, mp)][:].bitcast(F32)
-                for cl in range(3):
-                    c = 3 * sec + cl
-                    xt = pst.tile([P, 2, 2, P], F32, name="xt", tag="bank")
-                    for mi in range(2):
-                        for u in range(2):
-                            nc.tensor.transpose(
-                                xt[:, mi, u, :],
-                                gf[:, mi, 256 * cl + 128 * u : 256 * cl + 128 * u + 128],
-                                ident[:],
-                            )
-                    gg = ggp.tile([P, 256, 4], BF16, name="gg", tag="gg", align_bytes=64)
-                    copy_on(
-                        evac_count[0] % 3 == 2,
-                        gg[:].bitcast(F32).rearrange("p (m t) u -> p m t u", m=2),
-                        xt[:].rearrange("p m u t -> p m t u"),
+        def g_transpose(sec, mp, cl):
+            gf = g_tiles[(sec, mp)][:].bitcast(F32)
+            xt = psum.tile([P, 2, 2, P], F32, name="xt", tag="bank")
+            for mi in range(2):
+                for u in range(2):
+                    nc.tensor.transpose(
+                        xt[:, mi, u, :],
+                        gf[:, mi, 256 * cl + 128 * u : 256 * cl + 128 * u + 128],
+                        ident[:],
                     )
-                    evac_count[0] += 1
-                    nc.vector.quantize_mx(
-                        out=gq[:, c, 256 * mp : 256 * mp + 256].bitcast(E5M2X4),
-                        scales=gs[:, c, 256 * mp : 256 * mp + 256],
-                        in_=gg[:].rearrange("p t j -> p (t j)"),
-                    )
+            gg = ggp.tile([P, 256, 4], BF16, name="gg", tag="gg", align_bytes=64)
+            nc.scalar.copy(
+                out=gg[:].bitcast(F32).rearrange("p (m t) u -> p m t u", m=2),
+                in_=xt[:].rearrange("p m u t -> p m t u"),
+            )
+            gg_tiles[(sec, mp, cl)] = gg
 
-        def b_section(which):
+        def g_quant(sec, mp, cl):
+            c = 3 * sec + cl
+            nc.vector.quantize_mx(
+                out=gq[:, c, 256 * mp : 256 * mp + 256].bitcast(E5M2X4),
+                scales=gs[:, c, 256 * mp : 256 * mp + 256],
+                in_=gg_tiles[(sec, mp, cl)][:].rearrange("p t j -> p (t j)"),
+            )
+
+        def b_regroup(which):
             for cl in range(3):
-                j = 3 * which + cl
-                regroup(True, bgrp[:, j], braw[:, j])
+                regroup(True, bgrp[:, 3 * which + cl], braw[:, 3 * which + cl])
+
+        def b_quant(which):
             for cl in range(3):
                 j = 3 * which + cl
                 nc.vector.quantize_mx(
@@ -164,123 +156,150 @@ def tile_kvlora_kernel(tc, x, W, b, A1, B1, A2, B2, grad_out, out):
                     in_=bgrp[:, j].rearrange("p r t -> p (r t)"),
                 )
 
-        plain_ops = {}
-
         def lora_mx(which):
-            tt = pst.tile([P, TOK], F32, name="tt", tag="bank")
+            tt = psum.tile([P, TOK], F32, name="tt", tag="bank")
             for cl in range(3):
                 j = 3 * which + cl
-                c = 3 + j
                 nc.tensor.matmul_mx(
                     out=tt[:],
                     lhsT=bq[:, j, :].bitcast(E4M3X4),
                     lhsT_scale=bs[:, j, :],
-                    rhs=gq[:, c, :].bitcast(E5M2X4),
-                    rhs_scale=gs[:, c, :],
+                    rhs=gq[:, 3 + j, :].bitcast(E5M2X4),
+                    rhs_scale=gs[:, 3 + j, :],
                     start=(cl == 0),
                     stop=(cl == 2),
                 )
-            if HILO:
-                thi = keep.tile([P, TOK], BF16, name="thi%d" % which)
-                tlo = keep.tile([P, TOK], BF16, name="tlo%d" % which)
-                nc.scalar.copy(out=thi[:], in_=tt[:])
-                nc.vector.tensor_tensor(out=tlo[:], in0=tt[:], in1=thi[:], op=SUB)
-                plain_ops[which] = [(thi, ab[:, which, :]), (tlo, ab[:, which, :])]
-            else:
-                tsb = keep.tile([P, TOK], F32, name="tsb%d" % which)
-                nc.vector.tensor_copy(out=tsb[:, 0:P], in_=tt[:, 0:P])
-                nc.vector.tensor_copy(out=tsb[:, P:TOK], in_=tt[:, P:TOK])
-                plain_ops[which] = [(tsb, af[:, which, :])]
+            nc.vector.tensor_copy(out=tsb[:, which, 0:P], in_=tt[:, 0:P])
+            nc.vector.tensor_copy(out=tsb[:, which, P:TOK], in_=tt[:, P:TOK])
 
-        def plain_part(ps, which, m, n, first, last):
-            ops = plain_ops[which]
-            for idx, (lt, rt) in enumerate(ops):
-                nc.tensor.matmul(
-                    ps[:],
-                    lhsT=lt[:, P * m : P * m + P],
-                    rhs=rt[:, N_TILE * n : N_TILE * n + N_TILE],
-                    start=(first and idx == 0),
-                    stop=(last and idx == len(ops) - 1),
-                )
+        def plain_part(ps, which, m, n):
+            nc.tensor.matmul(
+                ps[:],
+                lhsT=tsb[:, which, P * m : P * m + P],
+                rhs=af[:, which, N_TILE * n : N_TILE * n + N_TILE],
+                start=(which == 0),
+                stop=(which == 1),
+            )
 
         def plain_evac(ps, m, n):
             nc.scalar.copy(out=lora[:, m, N_TILE * n : N_TILE * n + N_TILE], in_=ps[:])
 
-        def plain_tile(m, n):
-            ps = pst.tile([P, N_TILE], F32, name="ps", tag="bank")
-            plain_part(ps, 0, m, n, True, False)
-            plain_part(ps, 1, m, n, False, True)
+        def plain_tile(j):
+            m, n = j % M_TILES, j // M_TILES
+            ps = psum.tile([P, N_TILE], F32, name="ps", tag="bank")
+            plain_part(ps, 0, m, n)
+            plain_part(ps, 1, m, n)
             plain_evac(ps, m, n)
 
-        g_section(1)
-        b_section(0)
+        def chain(sec, which, between):
+            for mp in range(2):
+                for cl in range(3):
+                    g_transpose(sec, mp, cl)
+                    g_quant(sec, mp, cl)
+                    if mp == 1 and cl == 0:
+                        b_quant(which)
+                if mp == 0:
+                    between()
+                    b_regroup(which)
+
+        load_g(1, 0)
+        load_g(1, 1)
+        load_b(0, B1)
+        load_a(0, A1, 0, N_TILE)
+        load_g(2, 0)
+
+        def more_loads():
+            load_g(2, 1)
+            load_b(1, B2)
+            load_a(1, A2, 0, N_TILE)
+            load_a(0, A1, N_TILE, D)
+            load_a(1, A2, N_TILE, D)
+            for i in range(W_BUFS):
+                load_w(i)
+
+        def no_loads():
+            return None
+
+        chain(1, 0, more_loads)
         cast_a(0, 0)
         lora_mx(0)
+        chain(2, 1, no_loads)
         load_g(0, 0)
         load_g(0, 1)
-        g_section(2)
-        b_section(1)
         cast_a(1, 0)
-        lora_mx(1)
-        ps0 = []
-        for m in range(M_TILES):
-            ps = psa.tile([P, N_TILE], F32, name="ps0", tag="bank")
-            plain_part(ps, 0, m, 0, True, False)
-            ps0.append(ps)
-        for m in range(M_TILES):
-            plain_part(ps0[m], 1, m, 0, False, True)
-            plain_evac(ps0[m], m, 0)
         for n in range(1, N_BLOCKS):
             cast_a(0, n)
             cast_a(1, n)
+        ps0 = []
+        for m in range(M_TILES):
+            ps0.append(psum.tile([P, N_TILE], F32, name="ps0", tag="bank"))
+            plain_part(ps0[m], 0, m, 0)
+            if m == 1:
+                lora_mx(1)
+        for m in range(M_TILES):
+            plain_part(ps0[m], 1, m, 0)
 
-        n_pieces = len(pieces)
         grp_tiles = {}
 
-        def stage_regroup(i):
-            wg = wgrpp.tile([P, N_TILE, 4], BF16, name="wg", tag="wg", align_bytes=64)
-            regroup(i % 2 == 0, wg[:], w_tiles[i][:])
-            grp_tiles[i] = wg
-            if i + W_BUFS < n_pieces:
-                load_w(i + W_BUFS)
+        def main_tile(j):
+            n, m = j // M_TILES, j % M_TILES
+            acc = psum.tile([P, N_TILE], F32, name="acc", tag="bank")
+            for k in range(PASSES):
+                i = PASSES * n + k
+                c = pieces[i][1]
+                nc.tensor.matmul_mx(
+                    out=acc[:],
+                    lhsT=gq[:, c, P * m : P * m + P].bitcast(E5M2X4),
+                    lhsT_scale=gs[:, c, P * m : P * m + P],
+                    rhs=wq[:, i, :].bitcast(E4M3X4),
+                    rhs_scale=ws[:, i, :],
+                    start=(k == 0),
+                    stop=(k == PASSES - 1),
+                )
+            halves = 2 if j == N_BLOCKS * M_TILES - 1 else 1
+            wdt = N_TILE // halves
+            for h in range(halves):
+                lo = N_TILE * n + wdt * h
+                sl = lora[:, m, lo : lo + wdt]
+                nc.vector.tensor_tensor(out=sl, in0=acc[:, wdt * h : wdt * h + wdt], in1=sl, op=ADD)
+                nc.sync.dma_start(out=o2[P * m : P * m + P, lo : lo + wdt], in_=sl)
 
-        def stage_quant(i):
-            nc.vector.quantize_mx(
-                out=wq[:, i, :].bitcast(E4M3X4),
-                scales=ws[:, i, :],
-                in_=grp_tiles[i][:].rearrange("p w t -> p (w t)"),
-            )
+        def extras(i):
+            if i == 1:
+                plain_evac(ps0[0], 0, 0)
+                plain_evac(ps0[1], 1, 0)
+            if i == 3:
+                plain_evac(ps0[2], 2, 0)
+                plain_evac(ps0[3], 3, 0)
+                plain_tile(4)
+                plain_tile(5)
+                for mp in range(2):
+                    for cl in range(3):
+                        g_transpose(0, mp, cl)
+            if i == 7:
+                for mp in range(2):
+                    for cl in range(3):
+                        g_quant(0, mp, cl)
+            if i in (8, 11, 13):
+                first = {8: 6, 11: 8, 13: 10}[i]
+                plain_tile(first)
+                plain_tile(first + 1)
+            if i >= 19 and i % 2 == 1 and i <= 25:
+                main_tile((i - 19) // 2)
 
-        rest = [(m, n) for n in range(1, N_BLOCKS) for m in range(M_TILES)]
-        for i in range(n_pieces + 1):
-            if i == 4:
-                g_section(0)
+        for i in range(n_pieces + Q_LAG):
             if i < n_pieces:
-                stage_regroup(i)
-            if i >= 1:
-                stage_quant(i - 1)
-            if i % 2 == 1 and i // 2 < len(rest):
-                plain_tile(rest[i // 2][0], rest[i // 2][1])
-
-        for n in range(N_BLOCKS):
-            for m in range(M_TILES):
-                acc = psa.tile([P, N_TILE], F32, name="acc", tag="bank")
-                for k in range(PASSES):
-                    i = PASSES * n + k
-                    c = pieces[i][1]
-                    nc.tensor.matmul_mx(
-                        out=acc[:],
-                        lhsT=gq[:, c, P * m : P * m + P].bitcast(E5M2X4),
-                        lhsT_scale=gs[:, c, P * m : P * m + P],
-                        rhs=wq[:, i, :].bitcast(E4M3X4),
-                        rhs_scale=ws[:, i, :],
-                        start=(k == 0),
-                        stop=(k == PASSES - 1),
-                    )
-                halves = 2 if (n == N_BLOCKS - 1 and m == M_TILES - 1) else 1
-                wdt = N_TILE // halves
-                for h in range(halves):
-                    lo = N_TILE * n + wdt * h
-                    sl = lora[:, m, lo : lo + wdt]
-                    nc.vector.tensor_tensor(out=sl, in0=acc[:, wdt * h : wdt * h + wdt], in1=sl, op=ADD)
-                    nc.sync.dma_start(out=o2[P * m : P * m + P, lo : lo + wdt], in_=sl)
+                wg = wgrpp.tile([P, N_TILE, 4], BF16, name="wg", tag="wg", align_bytes=64)
+                regroup(not on_scalar(i), wg[:], w_tiles[i][:])
+                grp_tiles[i] = wg
+                if i + W_BUFS < n_pieces:
+                    load_w(i + W_BUFS)
+            if i >= Q_LAG:
+                nc.vector.quantize_mx(
+                    out=wq[:, i - Q_LAG, :].bitcast(E4M3X4),
+                    scales=ws[:, i - Q_LAG, :],
+                    in_=grp_tiles[i - Q_LAG][:].rearrange("p w t -> p (w t)"),
+                )
+            extras(i)
+        for j in range(4, N_BLOCKS * M_TILES):
+            main_tile(j)

@@ -75,14 +75,15 @@ def tile_kvlora_kernel(tc, x, W, b, A1, B1, A2, B2, grad_out, out):
 
         g_tiles = {}
 
-        def load_g(sec, mp):
+        def load_g(sec, mp, cuts=(0, SEC)):
             gt = gin.tile([P, 2, SEC], BF16, name="gt", tag="gt")
-            nc.sync.dma_start(
-                out=gt[:],
-                in_=g2[256 * mp : 256 * mp + 256, SEC * sec : SEC * sec + SEC].rearrange(
-                    "(m p) c -> p m c", p=P
-                ),
-            )
+            for lo, hi in zip(cuts[:-1], cuts[1:]):
+                nc.sync.dma_start(
+                    out=gt[:, :, lo:hi],
+                    in_=g2[256 * mp : 256 * mp + 256, SEC * sec + lo : SEC * sec + hi].rearrange(
+                        "(m p) c -> p m c", p=P
+                    ),
+                )
             g_tiles[(sec, mp)] = gt
 
         def load_b(which, bmat):
@@ -203,7 +204,7 @@ def tile_kvlora_kernel(tc, x, W, b, A1, B1, A2, B2, grad_out, out):
                     b_regroup(which)
 
         load_g(1, 0)
-        load_g(1, 1)
+        load_g(1, 1, (0, 2 * K_PASS, SEC))
         load_b(0, B1)
         load_a(0, A1, 0, N_TILE)
         load_g(2, 0)
@@ -217,24 +218,28 @@ def tile_kvlora_kernel(tc, x, W, b, A1, B1, A2, B2, grad_out, out):
             for i in range(W_BUFS):
                 load_w(i)
 
-        def no_loads():
-            return None
+        ps0 = []
+
+        def k_part(m):
+            ps0.append(psum.tile([P, N_TILE], F32, name="ps0", tag="bank"))
+            plain_part(ps0[m], 0, m, 0)
+
+        def first_k_part():
+            k_part(0)
 
         chain(1, 0, more_loads)
         cast_a(0, 0)
         lora_mx(0)
-        chain(2, 1, no_loads)
+        chain(2, 1, first_k_part)
         load_g(0, 0)
         load_g(0, 1)
         cast_a(1, 0)
         for n in range(1, N_BLOCKS):
             cast_a(0, n)
             cast_a(1, n)
-        ps0 = []
-        for m in range(M_TILES):
-            ps0.append(psum.tile([P, N_TILE], F32, name="ps0", tag="bank"))
-            plain_part(ps0[m], 0, m, 0)
-            if m == 1:
+        for m in range(1, M_TILES):
+            k_part(m)
+            if m == 2:
                 lora_mx(1)
         for m in range(M_TILES):
             plain_part(ps0[m], 1, m, 0)

@@ -49,8 +49,17 @@ def tile_kvlora_kernel(tc, x, W, b, A1, B1, A2, B2, grad_out, out):
         wgrpp = ctx.enter_context(tc.tile_pool(name="wgrpp", bufs=Q_LAG + 2))
         psum = ctx.enter_context(tc.psum_pool(name="psum", bufs=8))
 
+        warm = keep.tile([P, N_TILE], BF16, name="warm")
+        nc.vector.memset(warm[:], 0.0)
         ident = keep.tile([P, P], F32, name="ident")
         make_identity(nc, ident[:])
+        warm_ps = psum.tile([P, N_TILE], F32, name="warm_ps", tag="bank")
+
+        def keep_clock(count):
+            for rep in range(count):
+                nc.tensor.matmul(warm_ps[:], lhsT=warm[:, 0:P], rhs=warm[:], start=True, stop=True)
+
+        keep_clock(8)
 
         gq = keep.tile([P, PASSES, TOK], U32, name="gq", align_bytes=64)
         gs = keep.tile([P, PASSES, TOK], U8, name="gs", align_bytes=64)
@@ -217,6 +226,7 @@ def tile_kvlora_kernel(tc, x, W, b, A1, B1, A2, B2, grad_out, out):
             load_a(1, A2, N_TILE, D)
             for i in range(W_BUFS):
                 load_w(i)
+            keep_clock(3)
 
         ps0 = []
 
@@ -228,6 +238,7 @@ def tile_kvlora_kernel(tc, x, W, b, A1, B1, A2, B2, grad_out, out):
             k_part(0)
 
         chain(1, 0, more_loads)
+        keep_clock(3)
         cast_a(0, 0)
         lora_mx(0)
         chain(2, 1, first_k_part)

@@ -25,7 +25,7 @@ PASSES = 9
 CHUNK_ORDER = (3, 4, 5, 6, 7, 8, 0, 1, 2)
 W_BUFS = 6
 Q_LAG = 3
-PINNED = True
+PINNED = False
 
 FLOPS = 2 * TOK * O * D + 2 * 2 * TOK * SEC * R + 2 * 2 * TOK * R * D
 BYTES = 2 * (O * D + TOK * O + 2 * R * D + 2 * SEC * R) + 4 * TOK * D
@@ -49,17 +49,8 @@ def tile_kvlora_kernel(tc, x, W, b, A1, B1, A2, B2, grad_out, out):
         wgrpp = ctx.enter_context(tc.tile_pool(name="wgrpp", bufs=Q_LAG + 2))
         psum = ctx.enter_context(tc.psum_pool(name="psum", bufs=8))
 
-        warm = keep.tile([P, N_TILE], BF16, name="warm")
-        nc.vector.memset(warm[:], 0.0)
         ident = keep.tile([P, P], F32, name="ident")
         make_identity(nc, ident[:])
-        warm_ps = psum.tile([P, N_TILE], F32, name="warm_ps", tag="bank")
-
-        def keep_clock(count):
-            for rep in range(count):
-                nc.tensor.matmul(warm_ps[:], lhsT=warm[:, 0:P], rhs=warm[:], start=True, stop=True)
-
-        keep_clock(8)
 
         gq = keep.tile([P, PASSES, TOK], U32, name="gq", align_bytes=64)
         gs = keep.tile([P, PASSES, TOK], U8, name="gs", align_bytes=64)
@@ -226,7 +217,6 @@ def tile_kvlora_kernel(tc, x, W, b, A1, B1, A2, B2, grad_out, out):
             load_a(1, A2, N_TILE, D)
             for i in range(W_BUFS):
                 load_w(i)
-            keep_clock(3)
 
         ps0 = []
 
@@ -238,7 +228,6 @@ def tile_kvlora_kernel(tc, x, W, b, A1, B1, A2, B2, grad_out, out):
             k_part(0)
 
         chain(1, 0, more_loads)
-        keep_clock(3)
         cast_a(0, 0)
         lora_mx(0)
         chain(2, 1, first_k_part)

@@ -25,7 +25,7 @@ PASSES = 9
 CHUNK_ORDER = (3, 4, 5, 6, 7, 8, 0, 1, 2)
 W_BUFS = 6
 Q_LAG = 3
-PINNED = False
+PINNED = True
 
 FLOPS = 2 * TOK * O * D + 2 * 2 * TOK * SEC * R + 2 * 2 * TOK * R * D
 BYTES = 2 * (O * D + TOK * O + 2 * R * D + 2 * SEC * R) + 4 * TOK * D
@@ -276,9 +276,8 @@ def tile_kvlora_kernel(tc, x, W, b, A1, B1, A2, B2, grad_out, out):
             if i == 3:
                 plain_evac(ps0[2], 2, 0)
                 plain_evac(ps0[3], 3, 0)
-                plain_tile(4)
-                plain_tile(5)
                 for mp in range(2):
+                    plain_tile(4 + mp)
                     for cl in range(3):
                         g_transpose(0, mp, cl)
             if i == 7:

from contextlib import ExitStack

import concourse.mybir as mybir
from concourse.masks import make_identity

F32 = mybir.dt.float32
BF16 = mybir.dt.bfloat16
U32 = mybir.dt.uint32
U8 = mybir.dt.uint8
E4M3X4 = mybir.dt.float8_e4m3fn_x4
E5M2X4 = mybir.dt.float8_e5m2_x4
ADD = mybir.AluOpType.add

P = 128
TOK = 512
O = 4608
D = 1536
R = 128
SEC = 1536
K_PASS = 512
N_TILE = 512
N_BLOCKS = 3
M_TILES = 4
PASSES = 9
CHUNK_ORDER = (3, 4, 5, 6, 7, 8, 0, 1, 2)
W_BUFS = 6
Q_LAG = 3
PINNED = True

FLOPS = 2 * TOK * O * D + 2 * 2 * TOK * SEC * R + 2 * 2 * TOK * R * D
BYTES = 2 * (O * D + TOK * O + 2 * R * D + 2 * SEC * R) + 4 * TOK * D


def on_scalar(i):
    return i % 5 in (1, 3)


def tile_kvlora_kernel(tc, x, W, b, A1, B1, A2, B2, grad_out, out):
    nc = tc.nc
    g2 = grad_out.flatten_outer_dims()
    o2 = out.flatten_outer_dims()
    with ExitStack() as ctx:
        if PINNED:
            ctx.enter_context(tc.manual_schedule())
        keep = ctx.enter_context(tc.tile_pool(name="keep", bufs=1))
        gin = ctx.enter_context(tc.tile_pool(name="gin", bufs=3))
        ggp = ctx.enter_context(tc.tile_pool(name="ggp", bufs=6))
        wrawp = ctx.enter_context(tc.tile_pool(name="wrawp", bufs=W_BUFS))
        wgrpp = ctx.enter_context(tc.tile_pool(name="wgrpp", bufs=Q_LAG + 2))
        psum = ctx.enter_context(tc.psum_pool(name="psum", bufs=8))

        ident = keep.tile([P, P], F32, name="ident")
        make_identity(nc, ident[:])

        gq = keep.tile([P, PASSES, TOK], U32, name="gq", align_bytes=64)
        gs = keep.tile([P, PASSES, TOK], U8, name="gs", align_bytes=64)
        wq = keep.tile([P, N_BLOCKS * PASSES, N_TILE], U32, name="wq", align_bytes=64)
        ws = keep.tile([P, N_BLOCKS * PASSES, N_TILE], U8, name="ws", align_bytes=64)
        braw = keep.tile([P, 6, 4, R], BF16, name="braw")
        bgrp = keep.tile([P, 6, R, 4], BF16, name="bgrp", align_bytes=64)
        bq = keep.tile([P, 6, R], U32, name="bq", align_bytes=64)
        bs = keep.tile([P, 6, R], U8, name="bs", align_bytes=64)
        ab = keep.tile([P, 2, D], BF16, name="ab")
        af = keep.tile([P, 2, D], F32, name="af")
        tsb = keep.tile([P, 2, TOK], F32, name="tsb")
        lora = keep.tile([P, M_TILES, D], F32, name="lora")

        def regroup(on_vector, dst, src):
            dv = dst.rearrange("p (c i) t -> p c t i", i=4)
            sv = src.rearrange("p t (c i) -> p c t i", i=4)
            if on_vector:
                nc.vector.tensor_copy(out=dv, in_=sv)
            else:
                nc.scalar.copy(out=dv, in_=sv)

        g_tiles = {}

        def load_g(sec, mp, cuts=(0, SEC)):
            gt = gin.tile([P, 2, SEC], BF16, name="gt", tag="gt")
            for lo, hi in zip(cuts[:-1], cuts[1:]):
                nc.sync.dma_start(
                    out=gt[:, :, lo:hi],
                    in_=g2[256 * mp : 256 * mp + 256, SEC * sec + lo : SEC * sec + hi].rearrange(
                        "(m p) c -> p m c", p=P
                    ),
                )
            g_tiles[(sec, mp)] = gt

        def load_b(which, bmat):
            nc.sync.dma_start(
                out=braw[:, 3 * which : 3 * which + 3].rearrange("p c (u e) r -> p (c u) (e r)", e=2),
                in_=bmat.rearrange("(cu p e) r -> p cu (e r)", p=P, e=2),
            )

        def load_a(which, amat, lo, hi):
            nc.sync.dma_start(out=ab[:, which, lo:hi], in_=amat[:, lo:hi])

        pieces = [(n, c) for n in range(N_BLOCKS) for c in CHUNK_ORDER]
        n_pieces = len(pieces)
        w_tiles = {}

        def load_w(i):
            n, c = pieces[i]
            wt = wrawp.tile([P, 4, N_TILE], BF16, name="wt", tag="wt")
            for e in range(2):
                nc.sync.dma_start(
                    out=wt[:, e::2, :],
                    in_=W[
                        K_PASS * c + e : K_PASS * (c + 1) : 2, N_TILE * n : N_TILE * (n + 1)
                    ].rearrange("(u p) w -> p u w", u=2),
                )
            w_tiles[i] = wt

        def cast_a(which, n):
            nc.scalar.copy(
                out=af[:, which, N_TILE * n : N_TILE * n + N_TILE],
                in_=ab[:, which, N_TILE * n : N_TILE * n + N_TILE],
            )

        gg_tiles = {}

        def g_transpose(sec, mp, cl):
            gf = g_tiles[(sec, mp)][:].bitcast(F32)
            xt = psum.tile([P, 2, 2, P], F32, name="xt", tag="bank")
            for mi in range(2):
                for u in range(2):
                    nc.tensor.transpose(
                        xt[:, mi, u, :],
                        gf[:, mi, 256 * cl + 128 * u : 256 * cl + 128 * u + 128],
                        ident[:],
                    )
            gg = ggp.tile([P, 256, 4], BF16, name="gg", tag="gg", align_bytes=64)
            nc.scalar.copy(
                out=gg[:].bitcast(F32).rearrange("p (m t) u -> p m t u", m=2),
                in_=xt[:].rearrange("p m u t -> p m t u"),
            )
            gg_tiles[(sec, mp, cl)] = gg

        def g_quant(sec, mp, cl):
            c = 3 * sec + cl
            nc.vector.quantize_mx(
                out=gq[:, c, 256 * mp : 256 * mp + 256].bitcast(E5M2X4),
                scales=gs[:, c, 256 * mp : 256 * mp + 256],
                in_=gg_tiles[(sec, mp, cl)][:].rearrange("p t j -> p (t j)"),
            )

        def b_regroup(which):
            for cl in range(3):
                regroup(True, bgrp[:, 3 * which + cl], braw[:, 3 * which + cl])

        def b_quant(which):
            for cl in range(3):
                j = 3 * which + cl
                nc.vector.quantize_mx(
                    out=bq[:, j, :].bitcast(E4M3X4),
                    scales=bs[:, j, :],
                    in_=bgrp[:, j].rearrange("p r t -> p (r t)"),
                )

        def lora_mx(which):
            tt = psum.tile([P, TOK], F32, name="tt", tag="bank")
            for cl in range(3):
                j = 3 * which + cl
                nc.tensor.matmul_mx(
                    out=tt[:],
                    lhsT=bq[:, j, :].bitcast(E4M3X4),
                    lhsT_scale=bs[:, j, :],
                    rhs=gq[:, 3 + j, :].bitcast(E5M2X4),
                    rhs_scale=gs[:, 3 + j, :],
                    start=(cl == 0),
                    stop=(cl == 2),
                )
            nc.vector.tensor_copy(out=tsb[:, which, 0:P], in_=tt[:, 0:P])
            nc.vector.tensor_copy(out=tsb[:, which, P:TOK], in_=tt[:, P:TOK])

        def plain_part(ps, which, m, n):
            nc.tensor.matmul(
                ps[:],
                lhsT=tsb[:, which, P * m : P * m + P],
                rhs=af[:, which, N_TILE * n : N_TILE * n + N_TILE],
                start=(which == 0),
                stop=(which == 1),
            )

        def plain_evac(ps, m, n):
            nc.scalar.copy(out=lora[:, m, N_TILE * n : N_TILE * n + N_TILE], in_=ps[:])

        def plain_tile(j):
            m, n = j % M_TILES, j // M_TILES
            ps = psum.tile([P, N_TILE], F32, name="ps", tag="bank")
            plain_part(ps, 0, m, n)
            plain_part(ps, 1, m, n)
            plain_evac(ps, m, n)

        def chain(sec, which, between):
            for mp in range(2):
                for cl in range(3):
                    g_transpose(sec, mp, cl)
                    g_quant(sec, mp, cl)
                    if mp == 1 and cl == 0:
                        b_quant(which)
                if mp == 0:
                    between()
                    b_regroup(which)

        load_g(1, 0)
        load_g(1, 1, (0, 2 * K_PASS, SEC))
        load_b(0, B1)
        load_a(0, A1, 0, N_TILE)
        load_g(2, 0)

        def more_loads():
            load_g(2, 1)
            load_b(1, B2)
            load_a(1, A2, 0, N_TILE)
            load_a(0, A1, N_TILE, D)
            load_a(1, A2, N_TILE, D)
            for i in range(W_BUFS):
                load_w(i)

        ps0 = []

        def k_part(m):
            ps0.append(psum.tile([P, N_TILE], F32, name="ps0", tag="bank"))
            plain_part(ps0[m], 0, m, 0)

        def first_k_part():
            k_part(0)

        chain(1, 0, more_loads)
        cast_a(0, 0)
        lora_mx(0)
        chain(2, 1, first_k_part)
        load_g(0, 0)
        load_g(0, 1)
        cast_a(1, 0)
        for n in range(1, N_BLOCKS):
            cast_a(0, n)
            cast_a(1, n)
        for m in range(1, M_TILES):
            k_part(m)
            if m == 2:
                lora_mx(1)
        for m in range(M_TILES):
            plain_part(ps0[m], 1, m, 0)

        grp_tiles = {}

        def main_tile(j):
            n, m = j // M_TILES, j % M_TILES
            acc = psum.tile([P, N_TILE], F32, name="acc", tag="bank")
            for k in range(PASSES):
                i = PASSES * n + k
                c = pieces[i][1]
                nc.tensor.matmul_mx(
                    out=acc[:],
                    lhsT=gq[:, c, P * m : P * m + P].bitcast(E5M2X4),
                    lhsT_scale=gs[:, c, P * m : P * m + P],
                    rhs=wq[:, i, :].bitcast(E4M3X4),
                    rhs_scale=ws[:, i, :],
                    start=(k == 0),
                    stop=(k == PASSES - 1),
                )
            halves = 2 if j == N_BLOCKS * M_TILES - 1 else 1
            wdt = N_TILE // halves
            for h in range(halves):
                lo = N_TILE * n + wdt * h
                sl = lora[:, m, lo : lo + wdt]
                nc.vector.tensor_tensor(out=sl, in0=acc[:, wdt * h : wdt * h + wdt], in1=sl, op=ADD)
                nc.sync.dma_start(out=o2[P * m : P * m + P, lo : lo + wdt], in_=sl)

        def extras(i):
            if i == 1:
                plain_evac(ps0[0], 0, 0)
                plain_evac(ps0[1], 1, 0)
            if i == 3:
                plain_evac(ps0[2], 2, 0)
                plain_evac(ps0[3], 3, 0)
                for mp in range(2):
                    plain_tile(4 + mp)
                    for cl in range(3):
                        g_transpose(0, mp, cl)
            if i == 7:
                for mp in range(2):
                    for cl in range(3):
                        g_quant(0, mp, cl)
            if i in (8, 11, 13):
                first = {8: 6, 11: 8, 13: 10}[i]
                plain_tile(first)
                plain_tile(first + 1)
            if i >= 19 and i % 2 == 1 and i <= 25:
                main_tile((i - 19) // 2)

        for i in range(n_pieces + Q_LAG):
            if i < n_pieces:
                wg = wgrpp.tile([P, N_TILE, 4], BF16, name="wg", tag="wg", align_bytes=64)
                regroup(not on_scalar(i), wg[:], w_tiles[i][:])
                grp_tiles[i] = wg
                if i + W_BUFS < n_pieces:
                    load_w(i + W_BUFS)
            if i >= Q_LAG:
                nc.vector.quantize_mx(
                    out=wq[:, i - Q_LAG, :].bitcast(E4M3X4),
                    scales=ws[:, i - Q_LAG, :],
                    in_=grp_tiles[i - Q_LAG][:].rearrange("p w t -> p (w t)"),
                )
            extras(i)
        for j in range(4, N_BLOCKS * M_TILES):
            main_tile(j)
